import numpy as np
import ml_dtypes


def mxq(x, axis, fmt="e4m3"):
    dtype, down = {"e4m3": (ml_dtypes.float8_e4m3fn, 7), "e5m2": (ml_dtypes.float8_e5m2, 14)}[fmt]
    v = np.moveaxis(np.asarray(x, np.float32).astype(ml_dtypes.bfloat16).astype(np.float64), axis, -1)
    blocks = v.reshape(v.shape[:-1] + (-1, 32))
    amax = np.abs(blocks).max(-1, keepdims=True)
    byte = np.maximum(np.where(amax > 0, np.frexp(amax)[1] - 1 + 127, 0) - down, 1)
    scale = np.exp2(byte - 127.0)
    codes = (blocks / scale).astype(np.float32).astype(dtype).astype(np.float64)
    return np.moveaxis((codes * scale).reshape(v.shape), -1, axis)


WIDE = False


def mx_kscale(k):
    if not WIDE:
        return np.ones(k)
    levels = np.array([20, -20, 10, -10, 0])
    a = np.random.permutation(np.resize(levels, k // 512 * 4)).reshape(k // 512, 4)
    idx = np.arange(k)
    return np.exp2(a[idx // 512, idx % 128 // 32])


BF16 = ml_dtypes.bfloat16


def bf(x):
    return np.asarray(x, np.float32).astype(BF16)


def f64(x):
    return np.asarray(x).astype(np.float64)


B, S, A, O, H, L = 1024, 1024, 128, 1920, 1024, 384
G = L + A


def sigmoid(v):
    return 1.0 / (1.0 + np.exp(-v))


def setup_inputs():
    u = mx_kscale(H)
    u3 = np.tile(u, 3)
    sample = bf(np.random.standard_normal((B, L)) * 1.1)
    prev_action = bf(np.random.standard_normal((B, A)))
    prev_state = bf(np.random.standard_normal((B, S)))
    wih0 = bf(np.random.standard_normal((3 * H, G)) / np.sqrt(G))
    whh = bf(np.random.standard_normal((3 * H, H)) / np.sqrt(H))
    bih = bf(np.random.standard_normal(3 * H) * 0.1)
    bhh = bf(np.random.standard_normal(3 * H) * 0.1)
    g = bf(np.random.standard_normal((B, H)) * np.exp2(np.random.randint(-12, 1, (B, 1))) * 32.0 * u)
    xg = np.concatenate([f64(sample), f64(prev_action)], axis=-1)
    gi = xg @ f64(wih0).T + f64(bih)
    gh = f64(prev_state) @ f64(whh).T + f64(bhh)
    r = sigmoid(gi[:, :H] + gh[:, :H])
    z = sigmoid(gi[:, H:2 * H] + gh[:, H:2 * H])
    ghn = gh[:, 2 * H:]
    n = np.tanh(gi[:, 2 * H:] + r * ghn)
    gates = np.concatenate([r, z, n], axis=1)
    return {"sample": sample,
            "prev_action": prev_action,
            "prev_state": prev_state,
            "gru_Wih": bf(f64(wih0) / u3[:, None]),
            "gru_Whh": whh,
            "gru_bih": bih,
            "gru_bhh": bhh,
            "gates": np.asarray(gates, np.float32),
            "gh_n": np.asarray(ghn, np.float32),
            "grad_out": g}


def reference(sample, prev_action, prev_state, gru_Wih, gru_Whh, gru_bih, gru_bhh, gates, gh_n, grad_out):
    g = f64(grad_out)
    hp = f64(prev_state)
    gt = f64(gates)
    r, z, n = gt[:, :H], gt[:, H:2 * H], gt[:, 2 * H:]
    dn = g * (1.0 - z) * (1.0 - n * n)
    dz = g * (hp - n) * z * (1.0 - z)
    dr = dn * f64(gh_n) * r * (1.0 - r)
    dgi = np.concatenate([dr, dz, dn], axis=1)
    w = f64(gru_Wih)[:, :L]
    return mxq(dgi, 1, "e5m2") @ mxq(w, 0, "e4m3")

@@ -1,0 +1,279 @@
+from contextlib import ExitStack
+
+import concourse.mybir as mybir
+from concourse.masks import make_identity
+
+F32 = mybir.dt.float32
+BF16 = mybir.dt.bfloat16
+U32 = mybir.dt.uint32
+U8 = mybir.dt.uint8
+I32 = mybir.dt.int32
+E4M3_X4 = mybir.dt.float8_e4m3fn_x4
+E5M2_X4 = mybir.dt.float8_e5m2_x4
+ALU = mybir.AluOpType
+ACT = mybir.ActivationFunctionType
+
+P = 128
+PACK = 4
+K_PASS = P * PACK
+B, H, L = 1024, 1024, 384
+GATES = 3
+TOKEN_TILES = B // P
+HALVES = H // K_PASS
+PASSES = GATES * HALVES
+N_MOVING = 512
+W_VECTOR_COLS = 256
+
+FLOPS = 2 * B * GATES * H * L
+BYTES = 4 * B * GATES * H + 4 * B * H + 2 * 2 * B * H + 2 * GATES * H * L + 4 * B * L
+
+
+def tile_rssm_pb_v_kernel(
+    tc,
+    sample,
+    prev_action,
+    prev_state,
+    gru_Wih,
+    gru_Whh,
+    gru_bih,
+    gru_bhh,
+    gates,
+    gh_n,
+    grad_out,
+    out,
+):
+    nc = tc.nc
+    with ExitStack() as ctx:
+        consts = ctx.enter_context(tc.tile_pool(name="consts", bufs=1))
+        weights = ctx.enter_context(tc.tile_pool(name="weights", bufs=1))
+        inputs = ctx.enter_context(tc.tile_pool(name="inputs", bufs=3))
+        work = ctx.enter_context(tc.tile_pool(name="work", bufs=2))
+        banks = ctx.enter_context(tc.psum_pool(name="banks", bufs=7))
+        sums = ctx.enter_context(tc.psum_pool(name="sums", bufs=1))
+        ctx.enter_context(tc.manual_schedule())
+
+        ident_f32 = consts.tile([P, P], F32)
+        make_identity(nc, ident_f32[:])
+        ident_bf16 = consts.tile([P, P], BF16)
+        make_identity(nc, ident_bf16[:])
+
+        w_raw = weights.tile([P, PASSES, PACK, L], BF16)
+        for c in range(PASSES):
+            nc.sync.dma_start(
+                out=w_raw[:, c],
+                in_=gru_Wih[c * K_PASS : (c + 1) * K_PASS, 0:L].rearrange("(t p) n -> p t n", p=P),
+            )
+        w_grouped = weights.tile([P, PASSES, L, PACK], BF16, align_bytes=64)
+        w_codes = weights.tile([P, PASSES * L + N_MOVING - L], U32, align_bytes=64)
+        w_scales = weights.tile([P, PASSES * L + N_MOVING - L], U8, align_bytes=64)
+        nc.vector.memset(w_codes[:, PASSES * L :].bitcast(I32), 0)
+        nc.vector.memset(w_scales[:, PASSES * L :].bitcast(I32), 0)
+
+        def regroup_weights(c):
+            nc.vector.tensor_copy(
+                out=w_grouped[:, c, 0:W_VECTOR_COLS, :],
+                in_=w_raw[:, c, :, 0:W_VECTOR_COLS].rearrange("p t n -> p n t"),
+            )
+            nc.scalar.copy(
+                out=w_grouped[:, c, W_VECTOR_COLS:L, :],
+                in_=w_raw[:, c, :, W_VECTOR_COLS:L].rearrange("p t n -> p n t"),
+            )
+
+        def quantise_weights(c):
+            for first, last in ((0, W_VECTOR_COLS), (W_VECTOR_COLS, L)):
+                nc.vector.quantize_mx(
+                    out=w_codes[:, c * L + first : c * L + last].bitcast(E4M3_X4),
+                    scales=w_scales[:, c * L + first : c * L + last],
+                    in_=w_grouped[:, c, first:last, :].rearrange("p n t -> p (n t)"),
+                )
+
+        loaded = {}
+        psum = {}
+        sbuf = {}
+
+        def load(i):
+            rows = slice(i * P, (i + 1) * P)
+            g_in = inputs.tile([P, H], BF16)
+            nc.sync.dma_start(out=g_in[:], in_=grad_out[rows, :])
+            n_in = inputs.tile([P, H], F32)
+            nc.sync.dma_start(out=n_in[:], in_=gates[rows, 2 * H : 3 * H])
+            z_in = inputs.tile([P, H], F32)
+            nc.sync.dma_start(out=z_in[:], in_=gates[rows, H : 2 * H])
+            hp_in = inputs.tile([P, H], BF16)
+            nc.sync.dma_start(out=hp_in[:], in_=prev_state[rows, :])
+            r_in = inputs.tile([P, H], F32)
+            nc.sync.dma_start(out=r_in[:], in_=gates[rows, 0:H])
+            ghn_in = inputs.tile([P, H], F32)
+            nc.sync.dma_start(out=ghn_in[:], in_=gh_n[rows, :])
+            loaded[i] = {"g": g_in, "n": n_in, "z": z_in, "hp": hp_in, "r": r_in, "ghn": ghn_in}
+
+        def transpose_f32(i, name):
+            for half in range(HALVES):
+                bank = banks.tile([P, PACK, P], F32, tag="bank")
+                for t in range(PACK):
+                    col = half * K_PASS + t * P
+                    nc.tensor.transpose(bank[:, t, :], loaded[i][name][:, col : col + P], ident_f32[:])
+                psum[i, name, half] = bank[:]
+
+        def transpose_bf16(i, name):
+            bank = banks.tile([P, HALVES * PACK, P], BF16, tag="bank")
+            for chunk in range(HALVES * PACK):
+                nc.tensor.transpose(
+                    bank[:, chunk, :], loaded[i][name][:, chunk * P : (chunk + 1) * P], ident_bf16[:]
+                )
+            for half in range(HALVES):
+                psum[i, name, half] = bank[:, half * PACK : (half + 1) * PACK, :]
+
+        def from_psum(i, name, half):
+            return psum[i, name, half].rearrange("p t b -> p b t")
+
+        def new_tile(i, name, dtype):
+            made = work.tile([P, HALVES, P, PACK], dtype, tag=name, name=name)
+            sbuf[i, name] = made
+            return made
+
+        def whole(i, name):
+            return sbuf[i, name][:].rearrange("p h b t -> p (h b t)")
+
+        def transposes_for_scalar(i):
+            transpose_bf16(i, "g")
+            transpose_f32(i, "n")
+
+        def evacuate(i):
+            g_t = new_tile(i, "g_t", BF16)
+            n_t = new_tile(i, "n_t", F32)
+            for half in range(HALVES):
+                nc.scalar.copy(out=g_t[:, half], in_=from_psum(i, "g", half))
+            for half in range(HALVES):
+                nc.scalar.copy(out=n_t[:, half], in_=from_psum(i, "n", half))
+            new_tile(i, "n_sq", F32)
+            nc.scalar.activation(out=whole(i, "n_sq"), in_=whole(i, "n_t"), func=ACT.Square)
+
+        def transposes_for_vector(i):
+            transpose_f32(i, "z")
+            transpose_bf16(i, "hp")
+            transpose_f32(i, "r")
+            transpose_f32(i, "ghn")
+
+        def negate_r(i):
+            r_neg = new_tile(i, "r_neg", F32)
+            for half in range(HALVES):
+                nc.scalar.mul(out=r_neg[:, half], in_=from_psum(i, "r", half), mul=-1.0)
+
+        def products_of_z(i):
+            a_neg = new_tile(i, "a_neg", F32)
+            zt_neg = new_tile(i, "zt_neg", F32)
+            u_neg = new_tile(i, "u_neg", F32)
+            for half in range(HALVES):
+                nc.vector.scalar_tensor_tensor(
+                    out=a_neg[:, half],
+                    in0=from_psum(i, "z", half),
+                    scalar=1.0,
+                    in1=sbuf[i, "g_t"][:, half],
+                    op0=ALU.subtract,
+                    op1=ALU.mult,
+                )
+            for half in range(HALVES):
+                nc.vector.tensor_tensor(
+                    out=zt_neg[:, half], in0=from_psum(i, "z", half), in1=a_neg[:, half], op=ALU.mult
+                )
+            for half in range(HALVES):
+                nc.vector.tensor_tensor(
+                    out=u_neg[:, half],
+                    in0=sbuf[i, "n_t"][:, half],
+                    in1=from_psum(i, "hp", half),
+                    op=ALU.subtract,
+                )
+            dgi = work.tile([P, GATES, HALVES * K_PASS], BF16, align_bytes=64)
+            sbuf[i, "dgi"] = dgi
+            nc.gpsimd.tensor_tensor(out=dgi[:, 1, :], in0=whole(i, "zt_neg"), in1=whole(i, "u_neg"), op=ALU.mult)
+
+        def products_of_r(i):
+            r_term = new_tile(i, "r_term", F32)
+            q = new_tile(i, "q", F32)
+            for half in range(HALVES):
+                nc.vector.scalar_tensor_tensor(
+                    out=r_term[:, half],
+                    in0=from_psum(i, "r", half),
+                    scalar=1.0,
+                    in1=sbuf[i, "r_neg"][:, half],
+                    op0=ALU.subtract,
+                    op1=ALU.mult,
+                )
+            for half in range(HALVES):
+                nc.vector.tensor_tensor(
+                    out=q[:, half], in0=from_psum(i, "ghn", half), in1=r_term[:, half], op=ALU.mult
+                )
+            new_tile(i, "dn", F32)
+            nc.vector.scalar_tensor_tensor(
+                out=whole(i, "dn"),
+                in0=whole(i, "n_sq"),
+                scalar=1.0,
+                in1=whole(i, "a_neg"),
+                op0=ALU.subtract,
+                op1=ALU.mult,
+            )
+
+        def finish(i):
+            dgi = sbuf[i, "dgi"]
+            nc.scalar.copy(out=dgi[:, 2, :], in_=whole(i, "dn"))
+            nc.gpsimd.tensor_tensor(out=dgi[:, 0, :], in0=whole(i, "q"), in1=whole(i, "dn"), op=ALU.mult)
+
+        def quantise(i):
+            codes = work.tile([P, PASSES * P], U32, align_bytes=64)
+            scales = work.tile([P, PASSES * P], U8, align_bytes=64)
+            sbuf[i, "codes"] = codes
+            sbuf[i, "scales"] = scales
+            flat = sbuf[i, "dgi"][:].rearrange("p j c -> p (j c)")
+            for first, last in ((2 * HALVES * P, 3 * HALVES * P), (0, 2 * HALVES * P)):
+                nc.vector.quantize_mx(
+                    out=codes[:, first:last].bitcast(E5M2_X4),
+                    scales=scales[:, first:last],
+                    in_=flat[:, PACK * first : PACK * last],
+                )
+
+        def multiply(i):
+            acc = sums.tile([P, N_MOVING], F32)
+            for c in range(PASSES):
+                nc.tensor.matmul_mx(
+                    out=acc[:],
+                    lhsT=sbuf[i, "codes"][:, c * P : (c + 1) * P].bitcast(E5M2_X4),
+                    lhsT_scale=sbuf[i, "scales"][:, c * P : (c + 1) * P],
+                    rhs=w_codes[:, c * L : c * L + N_MOVING].bitcast(E4M3_X4),
+                    rhs_scale=w_scales[:, c * L : c * L + N_MOVING],
+                    start=(c == 0),
+                    stop=(c == PASSES - 1),
+                )
+            result = work.tile([P, L], F32)
+            nc.scalar.copy(out=result[:], in_=acc[:, 0:L])
+            nc.scalar.dma_start(out=out[i * P : (i + 1) * P, :], in_=result[:])
+
+        for i in range(3):
+            load(i)
+        for c in range(PASSES):
+            regroup_weights(c)
+            if c >= 1:
+                quantise_weights(c - 1)
+        quantise_weights(PASSES - 1)
+
+        transposes_for_scalar(0)
+        evacuate(0)
+        transposes_for_vector(0)
+        for i in range(TOKEN_TILES + 1):
+            if i + 3 < TOKEN_TILES:
+                load(i + 3)
+            if i >= 1:
+                finish(i - 1)
+            if i < TOKEN_TILES:
+                negate_r(i)
+                products_of_z(i)
+            if i + 1 < TOKEN_TILES:
+                transposes_for_scalar(i + 1)
+                evacuate(i + 1)
+            if i >= 1:
+                quantise(i - 1)
+                multiply(i - 1)
+            if i < TOKEN_TILES:
+                products_of_r(i)
+            if i + 1 < TOKEN_TILES:
+                transposes_for_vector(i + 1)

@@ -23,6 +23,7 @@ HALVES = H // K_PASS
 PASSES = GATES * HALVES
 N_MOVING = 512
 W_VECTOR_COLS = 256
+MX_RUN = 2
 
 FLOPS = 2 * B * GATES * H * L
 BYTES = 4 * B * GATES * H + 4 * B * H + 2 * 2 * B * H + 2 * GATES * H * L + 4 * B * L
@@ -56,6 +57,10 @@ def tile_rssm_pb_v_kernel(
         make_identity(nc, ident_f32[:])
         ident_bf16 = consts.tile([P, P], BF16)
         make_identity(nc, ident_bf16[:])
+        minus_half = consts.tile([P, 1], F32)
+        nc.vector.memset(minus_half[:], -0.5)
+        minus_quarter = consts.tile([P, 1], F32)
+        nc.vector.memset(minus_quarter[:], -0.25)
 
         w_raw = weights.tile([P, PASSES, PACK, L], BF16)
         for c in range(PASSES):
@@ -87,165 +92,169 @@ def tile_rssm_pb_v_kernel(
                     in_=w_grouped[:, c, first:last, :].rearrange("p n t -> p (n t)"),
                 )
 
-        loaded = {}
+        rows_first = {}
         psum = {}
-        sbuf = {}
+        k_first = {}
+
+        def live(i):
+            return 0 <= i < TOKEN_TILES
 
         def load(i):
             rows = slice(i * P, (i + 1) * P)
             g_in = inputs.tile([P, H], BF16)
             nc.sync.dma_start(out=g_in[:], in_=grad_out[rows, :])
-            n_in = inputs.tile([P, H], F32)
-            nc.sync.dma_start(out=n_in[:], in_=gates[rows, 2 * H : 3 * H])
             z_in = inputs.tile([P, H], F32)
             nc.sync.dma_start(out=z_in[:], in_=gates[rows, H : 2 * H])
             hp_in = inputs.tile([P, H], BF16)
             nc.sync.dma_start(out=hp_in[:], in_=prev_state[rows, :])
+            n_in = inputs.tile([P, H], F32)
+            nc.sync.dma_start(out=n_in[:], in_=gates[rows, 2 * H : 3 * H])
             r_in = inputs.tile([P, H], F32)
             nc.sync.dma_start(out=r_in[:], in_=gates[rows, 0:H])
             ghn_in = inputs.tile([P, H], F32)
             nc.sync.dma_start(out=ghn_in[:], in_=gh_n[rows, :])
-            loaded[i] = {"g": g_in, "n": n_in, "z": z_in, "hp": hp_in, "r": r_in, "ghn": ghn_in}
+            for name, made in (("g", g_in), ("z", z_in), ("hp", hp_in), ("n", n_in), ("r", r_in), ("ghn", ghn_in)):
+                rows_first[i, name] = made
 
-        def transpose_f32(i, name):
-            for half in range(HALVES):
-                bank = banks.tile([P, PACK, P], F32, tag="bank")
-                for t in range(PACK):
-                    col = half * K_PASS + t * P
-                    nc.tensor.transpose(bank[:, t, :], loaded[i][name][:, col : col + P], ident_f32[:])
-                psum[i, name, half] = bank[:]
+        def rows_first_tile(i, name):
+            made = work.tile([P, H], F32, tag=name, name=name)
+            rows_first[i, name] = made
+            return made
 
-        def transpose_bf16(i, name):
+        def r_term(i):
+            rt_neg = rows_first_tile(i, "rt_neg")
+            nc.scalar.activation(out=rt_neg[:], in_=rows_first[i, "r"][:], func=ACT.Square, bias=minus_half[:])
+            nc.scalar.activation(out=rt_neg[:], in_=rt_neg[:], func=ACT.Identity, bias=minus_quarter[:])
+
+        def square_n(i):
+            n_sq = rows_first_tile(i, "n_sq")
+            nc.scalar.activation(out=n_sq[:], in_=rows_first[i, "n"][:], func=ACT.Square)
+
+        def state_minus_n(i):
+            u = rows_first_tile(i, "u")
+            nc.gpsimd.tensor_tensor(out=u[:], in0=rows_first[i, "hp"][:], in1=rows_first[i, "n"][:], op=ALU.subtract)
+
+        def r_term_times_ghn(i):
+            q_neg = rows_first_tile(i, "q_neg")
+            nc.gpsimd.tensor_tensor(
+                out=q_neg[:], in0=rows_first[i, "rt_neg"][:], in1=rows_first[i, "ghn"][:], op=ALU.mult
+            )
+
+        def transpose_f32(i, name, half):
+            bank = banks.tile([P, PACK, P], F32, tag="bank")
+            for t in range(PACK):
+                col = half * K_PASS + t * P
+                nc.tensor.transpose(bank[:, t, :], rows_first[i, name][:, col : col + P], ident_f32[:])
+            psum[i, name, half] = bank[:]
+
+        def transpose_g(i):
             bank = banks.tile([P, HALVES * PACK, P], BF16, tag="bank")
             for chunk in range(HALVES * PACK):
                 nc.tensor.transpose(
-                    bank[:, chunk, :], loaded[i][name][:, chunk * P : (chunk + 1) * P], ident_bf16[:]
+                    bank[:, chunk, :], rows_first[i, "g"][:, chunk * P : (chunk + 1) * P], ident_bf16[:]
                 )
             for half in range(HALVES):
-                psum[i, name, half] = bank[:, half * PACK : (half + 1) * PACK, :]
+                psum[i, "g", half] = bank[:, half * PACK : (half + 1) * PACK, :]
 
         def from_psum(i, name, half):
             return psum[i, name, half].rearrange("p t b -> p b t")
 
-        def new_tile(i, name, dtype):
+        def k_first_tile(i, name, dtype):
             made = work.tile([P, HALVES, P, PACK], dtype, tag=name, name=name)
-            sbuf[i, name] = made
+            k_first[i, name] = made
             return made
 
-        def whole(i, name):
-            return sbuf[i, name][:].rearrange("p h b t -> p (h b t)")
-
-        def transposes_for_scalar(i):
-            transpose_bf16(i, "g")
-            transpose_f32(i, "n")
-
-        def evacuate(i):
-            g_t = new_tile(i, "g_t", BF16)
-            n_t = new_tile(i, "n_t", F32)
+        def negate_g(i):
+            g_neg = k_first_tile(i, "g_neg", BF16)
             for half in range(HALVES):
-                nc.scalar.copy(out=g_t[:, half], in_=from_psum(i, "g", half))
-            for half in range(HALVES):
-                nc.scalar.copy(out=n_t[:, half], in_=from_psum(i, "n", half))
-            new_tile(i, "n_sq", F32)
-            nc.scalar.activation(out=whole(i, "n_sq"), in_=whole(i, "n_t"), func=ACT.Square)
+                nc.scalar.mul(out=g_neg[:, half], in_=from_psum(i, "g", half), mul=-1.0)
 
-        def transposes_for_vector(i):
-            transpose_f32(i, "z")
-            transpose_bf16(i, "hp")
-            transpose_f32(i, "r")
-            transpose_f32(i, "ghn")
-
-        def negate_r(i):
-            r_neg = new_tile(i, "r_neg", F32)
-            for half in range(HALVES):
-                nc.scalar.mul(out=r_neg[:, half], in_=from_psum(i, "r", half), mul=-1.0)
-
-        def products_of_z(i):
-            a_neg = new_tile(i, "a_neg", F32)
-            zt_neg = new_tile(i, "zt_neg", F32)
-            u_neg = new_tile(i, "u_neg", F32)
+        def product_a(i):
+            a = k_first_tile(i, "a", F32)
             for half in range(HALVES):
                 nc.vector.scalar_tensor_tensor(
-                    out=a_neg[:, half],
+                    out=a[:, half],
                     in0=from_psum(i, "z", half),
                     scalar=1.0,
-                    in1=sbuf[i, "g_t"][:, half],
+                    in1=k_first[i, "g_neg"][:, half],
                     op0=ALU.subtract,
                     op1=ALU.mult,
                 )
-            for half in range(HALVES):
-                nc.vector.tensor_tensor(
-                    out=zt_neg[:, half], in0=from_psum(i, "z", half), in1=a_neg[:, half], op=ALU.mult
-                )
-            for half in range(HALVES):
-                nc.vector.tensor_tensor(
-                    out=u_neg[:, half],
-                    in0=sbuf[i, "n_t"][:, half],
-                    in1=from_psum(i, "hp", half),
-                    op=ALU.subtract,
-                )
-            dgi = work.tile([P, GATES, HALVES * K_PASS], BF16, align_bytes=64)
-            sbuf[i, "dgi"] = dgi
-            nc.gpsimd.tensor_tensor(out=dgi[:, 1, :], in0=whole(i, "zt_neg"), in1=whole(i, "u_neg"), op=ALU.mult)
 
-        def products_of_r(i):
-            r_term = new_tile(i, "r_term", F32)
-            q = new_tile(i, "q", F32)
+        def product_zt(i):
+            zt = k_first_tile(i, "zt", F32)
+            for half in range(HALVES):
+                nc.vector.tensor_tensor(
+                    out=zt[:, half], in0=from_psum(i, "z", half), in1=k_first[i, "a"][:, half], op=ALU.mult
+                )
+
+        def product_dz(i):
+            dgi = work.tile([P, GATES, HALVES, P, PACK], BF16, align_bytes=64)
+            k_first[i, "dgi"] = dgi
+            for half in range(HALVES):
+                nc.vector.tensor_tensor(
+                    out=dgi[:, 1, half], in0=from_psum(i, "u", half), in1=k_first[i, "zt"][:, half], op=ALU.mult
+                )
+
+        def product_dn(i):
+            dn_neg = k_first_tile(i, "dn_neg", F32)
             for half in range(HALVES):
                 nc.vector.scalar_tensor_tensor(
-                    out=r_term[:, half],
-                    in0=from_psum(i, "r", half),
+                    out=dn_neg[:, half],
+                    in0=from_psum(i, "n_sq", half),
                     scalar=1.0,
-                    in1=sbuf[i, "r_neg"][:, half],
+                    in1=k_first[i, "a"][:, half],
                     op0=ALU.subtract,
                     op1=ALU.mult,
                 )
-            for half in range(HALVES):
-                nc.vector.tensor_tensor(
-                    out=q[:, half], in0=from_psum(i, "ghn", half), in1=r_term[:, half], op=ALU.mult
-                )
-            new_tile(i, "dn", F32)
-            nc.vector.scalar_tensor_tensor(
-                out=whole(i, "dn"),
-                in0=whole(i, "n_sq"),
-                scalar=1.0,
-                in1=whole(i, "a_neg"),
-                op0=ALU.subtract,
-                op1=ALU.mult,
+
+        def round_dn(i):
+            nc.scalar.mul(
+                out=k_first[i, "dgi"][:, 2].rearrange("p h b t -> p (h b t)"),
+                in_=k_first[i, "dn_neg"][:].rearrange("p h b t -> p (h b t)"),
+                mul=-1.0,
             )
 
-        def finish(i):
-            dgi = sbuf[i, "dgi"]
-            nc.scalar.copy(out=dgi[:, 2, :], in_=whole(i, "dn"))
-            nc.gpsimd.tensor_tensor(out=dgi[:, 0, :], in0=whole(i, "q"), in1=whole(i, "dn"), op=ALU.mult)
+        def product_dr(i):
+            for half in range(HALVES):
+                nc.vector.tensor_tensor(
+                    out=k_first[i, "dgi"][:, 0, half],
+                    in0=from_psum(i, "q_neg", half),
+                    in1=k_first[i, "dn_neg"][:, half],
+                    op=ALU.mult,
+                )
 
         def quantise(i):
             codes = work.tile([P, PASSES * P], U32, align_bytes=64)
             scales = work.tile([P, PASSES * P], U8, align_bytes=64)
-            sbuf[i, "codes"] = codes
-            sbuf[i, "scales"] = scales
-            flat = sbuf[i, "dgi"][:].rearrange("p j c -> p (j c)")
-            for first, last in ((2 * HALVES * P, 3 * HALVES * P), (0, 2 * HALVES * P)):
+            k_first[i, "codes"] = codes
+            k_first[i, "scales"] = scales
+            flat = k_first[i, "dgi"][:].rearrange("p j h b t -> p (j h b t)")
+            for first, last in ((0, 2 * HALVES * P), (2 * HALVES * P, 3 * HALVES * P)):
                 nc.vector.quantize_mx(
                     out=codes[:, first:last].bitcast(E5M2_X4),
                     scales=scales[:, first:last],
                     in_=flat[:, PACK * first : PACK * last],
                 )
 
-        def multiply(i):
-            acc = sums.tile([P, N_MOVING], F32)
-            for c in range(PASSES):
+        def multiply(i, run):
+            if run == 0:
+                acc = sums.tile([P, N_MOVING], F32)
+                psum[i, "acc"] = acc
+            for c in range(run * MX_RUN, (run + 1) * MX_RUN):
                 nc.tensor.matmul_mx(
-                    out=acc[:],
-                    lhsT=sbuf[i, "codes"][:, c * P : (c + 1) * P].bitcast(E5M2_X4),
-                    lhsT_scale=sbuf[i, "scales"][:, c * P : (c + 1) * P],
+                    out=psum[i, "acc"][:],
+                    lhsT=k_first[i, "codes"][:, c * P : (c + 1) * P].bitcast(E5M2_X4),
+                    lhsT_scale=k_first[i, "scales"][:, c * P : (c + 1) * P],
                     rhs=w_codes[:, c * L : c * L + N_MOVING].bitcast(E4M3_X4),
                     rhs_scale=w_scales[:, c * L : c * L + N_MOVING],
                     start=(c == 0),
                     stop=(c == PASSES - 1),
                 )
+
+        def store(i):
             result = work.tile([P, L], F32)
-            nc.scalar.copy(out=result[:], in_=acc[:, 0:L])
+            nc.scalar.copy(out=result[:], in_=psum[i, "acc"][:, 0:L])
             nc.scalar.dma_start(out=out[i * P : (i + 1) * P, :], in_=result[:])
 
         for i in range(3):
@@ -256,24 +265,68 @@ def tile_rssm_pb_v_kernel(
                 quantise_weights(c - 1)
         quantise_weights(PASSES - 1)
 
-        transposes_for_scalar(0)
-        evacuate(0)
-        transposes_for_vector(0)
-        for i in range(TOKEN_TILES + 1):
-            if i + 3 < TOKEN_TILES:
+        transpose_g(0)
+        negate_g(0)
+        for half in range(HALVES):
+            transpose_f32(0, "z", half)
+        state_minus_n(0)
+        square_n(0)
+        r_term(0)
+        r_term_times_ghn(0)
+        state_minus_n(1)
+        for half in range(HALVES):
+            transpose_f32(0, "u", half)
+        for half in range(HALVES):
+            transpose_f32(0, "n_sq", half)
+        transpose_f32(0, "q_neg", 0)
+
+        for i in range(TOKEN_TILES + 2):
+            if live(i + 3):
                 load(i + 3)
-            if i >= 1:
-                finish(i - 1)
-            if i < TOKEN_TILES:
-                negate_r(i)
-                products_of_z(i)
-            if i + 1 < TOKEN_TILES:
-                transposes_for_scalar(i + 1)
-                evacuate(i + 1)
-            if i >= 1:
+            if live(i + 1):
+                r_term(i + 1)
+            if live(i):
+                product_a(i)
+            if live(i - 1):
                 quantise(i - 1)
-                multiply(i - 1)
-            if i < TOKEN_TILES:
-                products_of_r(i)
-            if i + 1 < TOKEN_TILES:
-                transposes_for_vector(i + 1)
+            if live(i + 1):
+                r_term_times_ghn(i + 1)
+            if live(i + 2):
+                state_minus_n(i + 2)
+            if live(i - 2):
+                store(i - 2)
+            if live(i + 1):
+                square_n(i + 1)
+
+            if live(i):
+                product_zt(i)
+                transpose_f32(i, "q_neg", 1)
+            if live(i + 1):
+                transpose_g(i + 1)
+                negate_g(i + 1)
+            if live(i - 1):
+                multiply(i - 1, 0)
+
+            if live(i):
+                product_dz(i)
+            if live(i + 1):
+                for half in range(HALVES):
+                    transpose_f32(i + 1, "z", half)
+            if live(i - 1):
+                multiply(i - 1, 1)
+
+            if live(i):
+                product_dn(i)
+                round_dn(i)
+            if live(i + 1):
+                for half in range(HALVES):
+                    transpose_f32(i + 1, "u", half)
+            if live(i - 1):
+                multiply(i - 1, 2)
+
+            if live(i):
+                product_dr(i)
+            if live(i + 1):
+                for half in range(HALVES):
+                    transpose_f32(i + 1, "n_sq", half)
+                transpose_f32(i + 1, "q_neg", 0)

@@ -23,7 +23,7 @@ HALVES = H // K_PASS
 PASSES = GATES * HALVES
 N_MOVING = 512
 W_VECTOR_COLS = 256
-MX_RUN = 2
+LAST = TOKEN_TILES - 1
 
 FLOPS = 2 * B * GATES * H * L
 BYTES = 4 * B * GATES * H + 4 * B * H + 2 * 2 * B * H + 2 * GATES * H * L + 4 * B * L
@@ -101,6 +101,8 @@ def tile_rssm_pb_v_kernel(
 
         def load(i):
             rows = slice(i * P, (i + 1) * P)
+            r_in = inputs.tile([P, H], F32)
+            nc.sync.dma_start(out=r_in[:], in_=gates[rows, 0:H])
             g_in = inputs.tile([P, H], BF16)
             nc.sync.dma_start(out=g_in[:], in_=grad_out[rows, :])
             z_in = inputs.tile([P, H], F32)
@@ -109,8 +111,6 @@ def tile_rssm_pb_v_kernel(
             nc.sync.dma_start(out=hp_in[:], in_=prev_state[rows, :])
             n_in = inputs.tile([P, H], F32)
             nc.sync.dma_start(out=n_in[:], in_=gates[rows, 2 * H : 3 * H])
-            r_in = inputs.tile([P, H], F32)
-            nc.sync.dma_start(out=r_in[:], in_=gates[rows, 0:H])
             ghn_in = inputs.tile([P, H], F32)
             nc.sync.dma_start(out=ghn_in[:], in_=gh_n[rows, :])
             for name, made in (("g", g_in), ("z", z_in), ("hp", hp_in), ("n", n_in), ("r", r_in), ("ghn", ghn_in)):
@@ -224,32 +224,35 @@ def tile_rssm_pb_v_kernel(
                     op=ALU.mult,
                 )
 
-        def quantise(i):
-            codes = work.tile([P, PASSES * P], U32, align_bytes=64)
-            scales = work.tile([P, PASSES * P], U8, align_bytes=64)
-            k_first[i, "codes"] = codes
-            k_first[i, "scales"] = scales
+        def quantise(i, first_gate, gate_count):
+            if (i, "codes") not in k_first:
+                codes = work.tile([P, PASSES * P], U32, align_bytes=64)
+                scales = work.tile([P, PASSES * P], U8, align_bytes=64)
+                k_first[i, "codes"] = codes
+                k_first[i, "scales"] = scales
+            first = first_gate * HALVES * P
+            last = (first_gate + gate_count) * HALVES * P
             flat = k_first[i, "dgi"][:].rearrange("p j h b t -> p (j h b t)")
-            for first, last in ((0, 2 * HALVES * P), (2 * HALVES * P, 3 * HALVES * P)):
-                nc.vector.quantize_mx(
-                    out=codes[:, first:last].bitcast(E5M2_X4),
-                    scales=scales[:, first:last],
-                    in_=flat[:, PACK * first : PACK * last],
-                )
+            nc.vector.quantize_mx(
+                out=k_first[i, "codes"][:, first:last].bitcast(E5M2_X4),
+                scales=k_first[i, "scales"][:, first:last],
+                in_=flat[:, PACK * first : PACK * last],
+            )
 
         def multiply(i, run):
+            gate = (run + 1) % GATES
             if run == 0:
                 acc = sums.tile([P, N_MOVING], F32)
                 psum[i, "acc"] = acc
-            for c in range(run * MX_RUN, (run + 1) * MX_RUN):
+            for c in range(gate * HALVES, (gate + 1) * HALVES):
                 nc.tensor.matmul_mx(
                     out=psum[i, "acc"][:],
                     lhsT=k_first[i, "codes"][:, c * P : (c + 1) * P].bitcast(E5M2_X4),
                     lhsT_scale=k_first[i, "scales"][:, c * P : (c + 1) * P],
                     rhs=w_codes[:, c * L : c * L + N_MOVING].bitcast(E4M3_X4),
                     rhs_scale=w_scales[:, c * L : c * L + N_MOVING],
-                    start=(c == 0),
-                    stop=(c == PASSES - 1),
+                    start=(run == 0 and c == gate * HALVES),
+                    stop=(run == GATES - 1 and c == (gate + 1) * HALVES - 1),
                 )
 
         def store(i):
@@ -270,8 +273,8 @@ def tile_rssm_pb_v_kernel(
         for half in range(HALVES):
             transpose_f32(0, "z", half)
         state_minus_n(0)
-        square_n(0)
         r_term(0)
+        square_n(0)
         r_term_times_ghn(0)
         state_minus_n(1)
         for half in range(HALVES):
@@ -280,53 +283,58 @@ def tile_rssm_pb_v_kernel(
             transpose_f32(0, "n_sq", half)
         transpose_f32(0, "q_neg", 0)
 
-        for i in range(TOKEN_TILES + 2):
+        for i in range(TOKEN_TILES):
             if live(i + 3):
                 load(i + 3)
             if live(i + 1):
                 r_term(i + 1)
-            if live(i):
-                product_a(i)
+            product_a(i)
             if live(i - 1):
-                quantise(i - 1)
+                quantise(i - 1, 0, 2)
+                quantise(i - 1, 2, 1)
             if live(i + 1):
                 r_term_times_ghn(i + 1)
             if live(i + 2):
                 state_minus_n(i + 2)
             if live(i - 2):
                 store(i - 2)
-            if live(i + 1):
-                square_n(i + 1)
 
-            if live(i):
-                product_zt(i)
-                transpose_f32(i, "q_neg", 1)
+            product_zt(i)
+            transpose_f32(i, "q_neg", 1)
             if live(i + 1):
                 transpose_g(i + 1)
                 negate_g(i + 1)
+                square_n(i + 1)
             if live(i - 1):
                 multiply(i - 1, 0)
 
-            if live(i):
-                product_dz(i)
+            product_dz(i)
             if live(i + 1):
                 for half in range(HALVES):
                     transpose_f32(i + 1, "z", half)
             if live(i - 1):
                 multiply(i - 1, 1)
 
-            if live(i):
-                product_dn(i)
-                round_dn(i)
+            product_dn(i)
+            round_dn(i)
             if live(i + 1):
                 for half in range(HALVES):
                     transpose_f32(i + 1, "u", half)
             if live(i - 1):
                 multiply(i - 1, 2)
+            if i == LAST:
+                quantise(i, 1, 1)
 
-            if live(i):
-                product_dr(i)
+            product_dr(i)
             if live(i + 1):
                 for half in range(HALVES):
                     transpose_f32(i + 1, "n_sq", half)
                 transpose_f32(i + 1, "q_neg", 0)
+
+        store(LAST - 1)
+        quantise(LAST, 2, 1)
+        multiply(LAST, 0)
+        multiply(LAST, 1)
+        quantise(LAST, 0, 1)
+        multiply(LAST, 2)
+        store(LAST)

@@ -239,6 +239,10 @@ def tile_rssm_pb_v_kernel(
                 in_=flat[:, PACK * first : PACK * last],
             )
 
+        def gpsimd_waits_for_quantise(i):
+            seen = work.tile([P, 1], U32)
+            nc.gpsimd.tensor_copy(out=seen[:], in_=k_first[i, "codes"][:, PASSES * P - 1 : PASSES * P])
+
         def multiply(i, run):
             gate = (run + 1) % GATES
             if run == 0:
@@ -276,7 +280,6 @@ def tile_rssm_pb_v_kernel(
         r_term(0)
         square_n(0)
         r_term_times_ghn(0)
-        state_minus_n(1)
         for half in range(HALVES):
             transpose_f32(0, "u", half)
         for half in range(HALVES):
@@ -289,17 +292,17 @@ def tile_rssm_pb_v_kernel(
             if live(i + 1):
                 r_term(i + 1)
             product_a(i)
-            if live(i - 1):
-                quantise(i - 1, 0, 2)
-                quantise(i - 1, 2, 1)
-            if live(i + 1):
-                r_term_times_ghn(i + 1)
-            if live(i + 2):
-                state_minus_n(i + 2)
             if live(i - 2):
                 store(i - 2)
 
             product_zt(i)
+            if live(i - 1):
+                quantise(i - 1, 0, 2)
+                quantise(i - 1, 2, 1)
+                gpsimd_waits_for_quantise(i - 1)
+            if live(i + 1):
+                state_minus_n(i + 1)
+                r_term_times_ghn(i + 1)
             transpose_f32(i, "q_neg", 1)
             if live(i + 1):
                 transpose_g(i + 1)

@@ -59,8 +59,8 @@ def tile_rssm_pb_v_kernel(
         make_identity(nc, ident_bf16[:])
         minus_half = consts.tile([P, 1], F32)
         nc.vector.memset(minus_half[:], -0.5)
-        minus_quarter = consts.tile([P, 1], F32)
-        nc.vector.memset(minus_quarter[:], -0.25)
+        plus_quarter = consts.tile([P, 1], F32)
+        nc.vector.memset(plus_quarter[:], 0.25)
 
         w_raw = weights.tile([P, PASSES, PACK, L], BF16)
         for c in range(PASSES):
@@ -124,7 +124,7 @@ def tile_rssm_pb_v_kernel(
         def r_term(i):
             rt_neg = rows_first_tile(i, "rt_neg")
             nc.scalar.activation(out=rt_neg[:], in_=rows_first[i, "r"][:], func=ACT.Square, bias=minus_half[:])
-            nc.scalar.activation(out=rt_neg[:], in_=rt_neg[:], func=ACT.Identity, bias=minus_quarter[:])
+            nc.scalar.activation(out=rt_neg[:], in_=rt_neg[:], func=ACT.Identity, bias=plus_quarter[:], scale=-1.0)
 
         def square_n(i):
             n_sq = rows_first_tile(i, "n_sq")
@@ -132,7 +132,7 @@ def tile_rssm_pb_v_kernel(
 
         def state_minus_n(i):
             u = rows_first_tile(i, "u")
-            nc.gpsimd.tensor_tensor(out=u[:], in0=rows_first[i, "hp"][:], in1=rows_first[i, "n"][:], op=ALU.subtract)
+            nc.gpsimd.tensor_tensor(out=u[:], in0=rows_first[i, "n"][:], in1=rows_first[i, "hp"][:], op=ALU.subtract)
 
         def r_term_times_ghn(i):
             q_neg = rows_first_tile(i, "q_neg")
@@ -153,8 +153,7 @@ def tile_rssm_pb_v_kernel(
                 nc.tensor.transpose(
                     bank[:, chunk, :], rows_first[i, "g"][:, chunk * P : (chunk + 1) * P], ident_bf16[:]
                 )
-            for half in range(HALVES):
-                psum[i, "g", half] = bank[:, half * PACK : (half + 1) * PACK, :]
+            psum[i, "g"] = bank[:]
 
         def from_psum(i, name, half):
             return psum[i, name, half].rearrange("p t b -> p b t")
@@ -166,8 +165,7 @@ def tile_rssm_pb_v_kernel(
 
         def negate_g(i):
             g_neg = k_first_tile(i, "g_neg", BF16)
-            for half in range(HALVES):
-                nc.scalar.mul(out=g_neg[:, half], in_=from_psum(i, "g", half), mul=-1.0)
+            nc.scalar.copy(out=g_neg[:], in_=psum[i, "g"].rearrange("p (h t) b -> p h b t", t=PACK))
 
         def product_a(i):
             a = k_first_tile(i, "a", F32)
@@ -209,10 +207,9 @@ def tile_rssm_pb_v_kernel(
                 )
 
         def round_dn(i):
-            nc.scalar.mul(
+            nc.scalar.copy(
                 out=k_first[i, "dgi"][:, 2].rearrange("p h b t -> p (h b t)"),
                 in_=k_first[i, "dn_neg"][:].rearrange("p h b t -> p (h b t)"),
-                mul=-1.0,
             )
 
         def product_dr(i):

@@ -63,11 +63,14 @@ def tile_rssm_pb_v_kernel(
         nc.vector.memset(plus_quarter[:], 0.25)
 
         w_raw = weights.tile([P, PASSES, PACK, L], BF16)
-        for c in range(PASSES):
-            nc.sync.dma_start(
-                out=w_raw[:, c],
-                in_=gru_Wih[c * K_PASS : (c + 1) * K_PASS, 0:L].rearrange("(t p) n -> p t n", p=P),
-            )
+
+        def load_weights():
+            for c in range(PASSES):
+                nc.sync.dma_start(
+                    out=w_raw[:, c],
+                    in_=gru_Wih[c * K_PASS : (c + 1) * K_PASS, 0:L].rearrange("(t p) n -> p t n", p=P),
+                )
+
         w_grouped = weights.tile([P, PASSES, L, PACK], BF16, align_bytes=64)
         w_codes = weights.tile([P, PASSES * L + N_MOVING - L], U32, align_bytes=64)
         w_scales = weights.tile([P, PASSES * L + N_MOVING - L], U8, align_bytes=64)
@@ -99,21 +102,20 @@ def tile_rssm_pb_v_kernel(
         def live(i):
             return 0 <= i < TOKEN_TILES
 
-        def load(i):
+        def load(i, order):
             rows = slice(i * P, (i + 1) * P)
-            r_in = inputs.tile([P, H], F32)
-            nc.sync.dma_start(out=r_in[:], in_=gates[rows, 0:H])
-            g_in = inputs.tile([P, H], BF16)
-            nc.sync.dma_start(out=g_in[:], in_=grad_out[rows, :])
-            z_in = inputs.tile([P, H], F32)
-            nc.sync.dma_start(out=z_in[:], in_=gates[rows, H : 2 * H])
-            hp_in = inputs.tile([P, H], BF16)
-            nc.sync.dma_start(out=hp_in[:], in_=prev_state[rows, :])
-            n_in = inputs.tile([P, H], F32)
-            nc.sync.dma_start(out=n_in[:], in_=gates[rows, 2 * H : 3 * H])
-            ghn_in = inputs.tile([P, H], F32)
-            nc.sync.dma_start(out=ghn_in[:], in_=gh_n[rows, :])
-            for name, made in (("g", g_in), ("z", z_in), ("hp", hp_in), ("n", n_in), ("r", r_in), ("ghn", ghn_in)):
+            sources = {
+                "r": (gates[rows, 0:H], F32),
+                "z": (gates[rows, H : 2 * H], F32),
+                "n": (gates[rows, 2 * H : 3 * H], F32),
+                "ghn": (gh_n[rows, :], F32),
+                "g": (grad_out[rows, :], BF16),
+                "hp": (prev_state[rows, :], BF16),
+            }
+            for name in order:
+                source, dtype = sources[name]
+                made = inputs.tile([P, H], dtype, tag=name, name=name)
+                nc.sync.dma_start(out=made[:], in_=source)
                 rows_first[i, name] = made
 
         def rows_first_tile(i, name):
@@ -186,15 +188,20 @@ def tile_rssm_pb_v_kernel(
                     out=zt[:, half], in0=from_psum(i, "z", half), in1=k_first[i, "a"][:, half], op=ALU.mult
                 )
 
+        def dgi_tile(i):
+            if (i, "dgi") not in k_first:
+                dgi = work.tile([P, GATES, HALVES, P, PACK], BF16, align_bytes=64)
+                k_first[i, "dgi"] = dgi
+
         def product_dz(i):
-            dgi = work.tile([P, GATES, HALVES, P, PACK], BF16, align_bytes=64)
-            k_first[i, "dgi"] = dgi
+            dgi_tile(i)
             for half in range(HALVES):
                 nc.vector.tensor_tensor(
-                    out=dgi[:, 1, half], in0=from_psum(i, "u", half), in1=k_first[i, "zt"][:, half], op=ALU.mult
+                    out=k_first[i, "dgi"][:, 1, half], in0=from_psum(i, "u", half), in1=k_first[i, "zt"][:, half], op=ALU.mult
                 )
 
         def product_dn(i):
+            dgi_tile(i)
             dn_neg = k_first_tile(i, "dn_neg", F32)
             for half in range(HALVES):
                 nc.vector.scalar_tensor_tensor(
@@ -261,8 +268,22 @@ def tile_rssm_pb_v_kernel(
             nc.scalar.copy(out=result[:], in_=psum[i, "acc"][:, 0:L])
             nc.scalar.dma_start(out=out[i * P : (i + 1) * P, :], in_=result[:])
 
-        for i in range(3):
-            load(i)
+        HEAD_ORDER = ("g", "z", "n", "hp", "r", "ghn")
+        LOOP_ORDER = ("r", "g", "z", "hp", "n", "ghn")
+
+        def transpose_both(i, name):
+            for half in range(HALVES):
+                transpose_f32(i, name, half)
+
+        def quantise_tile(i):
+            quantise(i, 0, 2)
+            quantise(i, 2, 1)
+            gpsimd_waits_for_quantise(i)
+
+        load_weights()
+        load(0, HEAD_ORDER)
+        load(1, HEAD_ORDER)
+        load(2, LOOP_ORDER)
         for c in range(PASSES):
             regroup_weights(c)
             if c >= 1:
@@ -271,32 +292,67 @@ def tile_rssm_pb_v_kernel(
 
         transpose_g(0)
         negate_g(0)
-        for half in range(HALVES):
-            transpose_f32(0, "z", half)
-        state_minus_n(0)
-        r_term(0)
+        transpose_both(0, "z")
         square_n(0)
+        transpose_both(0, "n_sq")
+        state_minus_n(0)
+        transpose_both(0, "u")
+        r_term(0)
         r_term_times_ghn(0)
-        for half in range(HALVES):
-            transpose_f32(0, "u", half)
-        for half in range(HALVES):
-            transpose_f32(0, "n_sq", half)
-        transpose_f32(0, "q_neg", 0)
+        product_a(0)
+        product_zt(0)
+        transpose_g(1)
+        product_dn(0)
+        round_dn(0)
+        negate_g(1)
+        transpose_both(1, "z")
+        transpose_both(0, "q_neg")
+        product_dz(0)
+        load(3, LOOP_ORDER)
+        state_minus_n(1)
+        transpose_both(1, "u")
+        square_n(1)
+        product_a(1)
+        product_zt(1)
+        transpose_both(1, "n_sq")
+        transpose_g(2)
+        product_dr(0)
+        r_term(1)
+        quantise_tile(0)
+        r_term_times_ghn(1)
+        transpose_both(1, "q_neg")
 
-        for i in range(TOKEN_TILES):
+        load(4, LOOP_ORDER)
+        r_term(2)
+        negate_g(2)
+        state_minus_n(2)
+        r_term_times_ghn(2)
+        multiply(0, 0)
+        product_dz(1)
+        transpose_both(2, "z")
+        multiply(0, 1)
+        product_dn(1)
+        round_dn(1)
+        square_n(2)
+        transpose_both(2, "u")
+        multiply(0, 2)
+        product_dr(1)
+        transpose_both(2, "n_sq")
+        transpose_f32(2, "q_neg", 0)
+
+        for i in range(2, TOKEN_TILES):
+            early = i == 2
             if live(i + 3):
-                load(i + 3)
+                load(i + 3, LOOP_ORDER)
             if live(i + 1):
                 r_term(i + 1)
             product_a(i)
-            if live(i - 2):
-                store(i - 2)
+            store(i - 2)
 
             product_zt(i)
-            if live(i - 1):
-                quantise(i - 1, 0, 2)
-                quantise(i - 1, 2, 1)
-                gpsimd_waits_for_quantise(i - 1)
+            if early:
+                product_dz(i)
+            quantise_tile(i - 1)
             if live(i + 1):
                 state_minus_n(i + 1)
                 r_term_times_ghn(i + 1)
@@ -305,33 +361,28 @@ def tile_rssm_pb_v_kernel(
                 transpose_g(i + 1)
                 negate_g(i + 1)
                 square_n(i + 1)
-            if live(i - 1):
-                multiply(i - 1, 0)
+            multiply(i - 1, 0)
 
-            product_dz(i)
+            if not early:
+                product_dz(i)
             if live(i + 1):
-                for half in range(HALVES):
-                    transpose_f32(i + 1, "z", half)
-            if live(i - 1):
-                multiply(i - 1, 1)
+                transpose_both(i + 1, "z")
+            multiply(i - 1, 1)
 
             product_dn(i)
-            round_dn(i)
             if live(i + 1):
-                for half in range(HALVES):
-                    transpose_f32(i + 1, "u", half)
-            if live(i - 1):
-                multiply(i - 1, 2)
+                transpose_both(i + 1, "u")
+            multiply(i - 1, 2)
             if i == LAST:
                 quantise(i, 1, 1)
+                store(i - 1)
+            round_dn(i)
 
             product_dr(i)
             if live(i + 1):
-                for half in range(HALVES):
-                    transpose_f32(i + 1, "n_sq", half)
+                transpose_both(i + 1, "n_sq")
                 transpose_f32(i + 1, "q_neg", 0)
 
-        store(LAST - 1)
         quantise(LAST, 2, 1)
         multiply(LAST, 0)
         multiply(LAST, 1)

@@ -57,6 +57,8 @@ def tile_rssm_pb_v_kernel(
         make_identity(nc, ident_f32[:])
         ident_bf16 = consts.tile([P, P], BF16)
         make_identity(nc, ident_bf16[:])
+        minus_ident_bf16 = consts.tile([P, P], BF16)
+        nc.scalar.mul(out=minus_ident_bf16[:], in_=ident_bf16[:], mul=-1.0)
         minus_half = consts.tile([P, 1], F32)
         nc.vector.memset(minus_half[:], -0.5)
         plus_quarter = consts.tile([P, 1], F32)
@@ -134,7 +136,11 @@ def tile_rssm_pb_v_kernel(
 
         def state_minus_n(i):
             u = rows_first_tile(i, "u")
-            nc.gpsimd.tensor_tensor(out=u[:], in0=rows_first[i, "n"][:], in1=rows_first[i, "hp"][:], op=ALU.subtract)
+            cols = slice(K_PASS, H)
+            nc.gpsimd.tensor_tensor(
+                out=u[:, cols], in0=rows_first[i, "n"][:, cols], in1=rows_first[i, "hp"][:, cols], op=ALU.subtract
+            )
+            nc.gpsimd.tensor_tensor(out=u[:, cols], in0=rows_first[i, "z"][:, cols], in1=u[:, cols], op=ALU.mult)
 
         def r_term_times_ghn(i):
             q_neg = rows_first_tile(i, "q_neg")
@@ -146,7 +152,24 @@ def tile_rssm_pb_v_kernel(
             bank = banks.tile([P, PACK, P], F32, tag="bank")
             for t in range(PACK):
                 col = half * K_PASS + t * P
-                nc.tensor.transpose(bank[:, t, :], rows_first[i, name][:, col : col + P], ident_f32[:])
+                if name == "u" and half == 0:
+                    nc.tensor.matmul(
+                        out=bank[:, t, :],
+                        lhsT=rows_first[i, "n"][:, col : col + P],
+                        rhs=ident_f32[:],
+                        is_transpose=True,
+                        start=True,
+                        stop=False,
+                    )
+                    nc.tensor.matmul(
+                        out=bank[:, t, :],
+                        lhsT=rows_first[i, "hp"][:, col : col + P],
+                        rhs=minus_ident_bf16[:],
+                        start=False,
+                        stop=True,
+                    )
+                else:
+                    nc.tensor.transpose(bank[:, t, :], rows_first[i, name][:, col : col + P], ident_f32[:])
             psum[i, name, half] = bank[:]
 
         def transpose_g(i):
@@ -183,7 +206,7 @@ def tile_rssm_pb_v_kernel(
 
         def product_zt(i):
             zt = k_first_tile(i, "zt", F32)
-            for half in range(HALVES):
+            for half in (0,):
                 nc.vector.tensor_tensor(
                     out=zt[:, half], in0=from_psum(i, "z", half), in1=k_first[i, "a"][:, half], op=ALU.mult
                 )
@@ -197,7 +220,7 @@ def tile_rssm_pb_v_kernel(
             dgi_tile(i)
             for half in range(HALVES):
                 nc.vector.tensor_tensor(
-                    out=k_first[i, "dgi"][:, 1, half], in0=from_psum(i, "u", half), in1=k_first[i, "zt"][:, half], op=ALU.mult
+                    out=k_first[i, "dgi"][:, 1, half], in0=from_psum(i, "u", half), in1=k_first[i, "zt" if half == 0 else "a"][:, half], op=ALU.mult
                 )
 
         def product_dn(i):

@@ -371,6 +371,8 @@ def tile_rssm_pb_v_kernel(
                 r_term(i + 1)
             product_a(i)
             store(i - 2)
+            if live(i + 1):
+                square_n(i + 1)
 
             product_zt(i)
             if early:
@@ -383,7 +385,6 @@ def tile_rssm_pb_v_kernel(
             if live(i + 1):
                 transpose_g(i + 1)
                 negate_g(i + 1)
-                square_n(i + 1)
             multiply(i - 1, 0)
 
             if not early:

from contextlib import ExitStack

import concourse.mybir as mybir
from concourse.masks import make_identity

F32 = mybir.dt.float32
BF16 = mybir.dt.bfloat16
U32 = mybir.dt.uint32
U8 = mybir.dt.uint8
I32 = mybir.dt.int32
E4M3_X4 = mybir.dt.float8_e4m3fn_x4
E5M2_X4 = mybir.dt.float8_e5m2_x4
ALU = mybir.AluOpType
ACT = mybir.ActivationFunctionType

P = 128
PACK = 4
K_PASS = P * PACK
B, H, L = 1024, 1024, 384
GATES = 3
TOKEN_TILES = B // P
HALVES = H // K_PASS
PASSES = GATES * HALVES
N_MOVING = 512
W_VECTOR_COLS = 256
LAST = TOKEN_TILES - 1

FLOPS = 2 * B * GATES * H * L
BYTES = 4 * B * GATES * H + 4 * B * H + 2 * 2 * B * H + 2 * GATES * H * L + 4 * B * L


def tile_rssm_pb_v_kernel(
    tc,
    sample,
    prev_action,
    prev_state,
    gru_Wih,
    gru_Whh,
    gru_bih,
    gru_bhh,
    gates,
    gh_n,
    grad_out,
    out,
):
    nc = tc.nc
    with ExitStack() as ctx:
        consts = ctx.enter_context(tc.tile_pool(name="consts", bufs=1))
        weights = ctx.enter_context(tc.tile_pool(name="weights", bufs=1))
        inputs = ctx.enter_context(tc.tile_pool(name="inputs", bufs=3))
        work = ctx.enter_context(tc.tile_pool(name="work", bufs=2))
        banks = ctx.enter_context(tc.psum_pool(name="banks", bufs=7))
        sums = ctx.enter_context(tc.psum_pool(name="sums", bufs=1))
        ctx.enter_context(tc.manual_schedule())

        ident_f32 = consts.tile([P, P], F32)
        make_identity(nc, ident_f32[:])
        ident_bf16 = consts.tile([P, P], BF16)
        make_identity(nc, ident_bf16[:])
        minus_ident_bf16 = consts.tile([P, P], BF16)
        nc.scalar.mul(out=minus_ident_bf16[:], in_=ident_bf16[:], mul=-1.0)
        minus_half = consts.tile([P, 1], F32)
        nc.vector.memset(minus_half[:], -0.5)
        plus_quarter = consts.tile([P, 1], F32)
        nc.vector.memset(plus_quarter[:], 0.25)

        w_raw = weights.tile([P, PASSES, PACK, L], BF16)

        def load_weights():
            for c in range(PASSES):
                nc.sync.dma_start(
                    out=w_raw[:, c],
                    in_=gru_Wih[c * K_PASS : (c + 1) * K_PASS, 0:L].rearrange("(t p) n -> p t n", p=P),
                )

        w_grouped = weights.tile([P, PASSES, L, PACK], BF16, align_bytes=64)
        w_codes = weights.tile([P, PASSES * L + N_MOVING - L], U32, align_bytes=64)
        w_scales = weights.tile([P, PASSES * L + N_MOVING - L], U8, align_bytes=64)
        nc.vector.memset(w_codes[:, PASSES * L :].bitcast(I32), 0)
        nc.vector.memset(w_scales[:, PASSES * L :].bitcast(I32), 0)

        def regroup_weights(c):
            nc.vector.tensor_copy(
                out=w_grouped[:, c, 0:W_VECTOR_COLS, :],
                in_=w_raw[:, c, :, 0:W_VECTOR_COLS].rearrange("p t n -> p n t"),
            )
            nc.scalar.copy(
                out=w_grouped[:, c, W_VECTOR_COLS:L, :],
                in_=w_raw[:, c, :, W_VECTOR_COLS:L].rearrange("p t n -> p n t"),
            )

        def quantise_weights(c):
            for first, last in ((0, W_VECTOR_COLS), (W_VECTOR_COLS, L)):
                nc.vector.quantize_mx(
                    out=w_codes[:, c * L + first : c * L + last].bitcast(E4M3_X4),
                    scales=w_scales[:, c * L + first : c * L + last],
                    in_=w_grouped[:, c, first:last, :].rearrange("p n t -> p (n t)"),
                )

        rows_first = {}
        psum = {}
        k_first = {}

        def live(i):
            return 0 <= i < TOKEN_TILES

        def load(i, order):
            rows = slice(i * P, (i + 1) * P)
            sources = {
                "r": (gates[rows, 0:H], F32),
                "z": (gates[rows, H : 2 * H], F32),
                "n": (gates[rows, 2 * H : 3 * H], F32),
                "ghn": (gh_n[rows, :], F32),
                "g": (grad_out[rows, :], BF16),
                "hp": (prev_state[rows, :], BF16),
            }
            for name in order:
                source, dtype = sources[name]
                made = inputs.tile([P, H], dtype, tag=name, name=name)
                nc.sync.dma_start(out=made[:], in_=source)
                rows_first[i, name] = made

        def rows_first_tile(i, name):
            made = work.tile([P, H], F32, tag=name, name=name)
            rows_first[i, name] = made
            return made

        def r_term(i):
            rt_neg = rows_first_tile(i, "rt_neg")
            nc.scalar.activation(out=rt_neg[:], in_=rows_first[i, "r"][:], func=ACT.Square, bias=minus_half[:])
            nc.scalar.activation(out=rt_neg[:], in_=rt_neg[:], func=ACT.Identity, bias=plus_quarter[:], scale=-1.0)

        def square_n(i):
            n_sq = rows_first_tile(i, "n_sq")
            nc.scalar.activation(out=n_sq[:], in_=rows_first[i, "n"][:], func=ACT.Square)

        def state_minus_n(i):
            u = rows_first_tile(i, "u")
            cols = slice(K_PASS, H)
            nc.gpsimd.tensor_tensor(
                out=u[:, cols], in0=rows_first[i, "n"][:, cols], in1=rows_first[i, "hp"][:, cols], op=ALU.subtract
            )
            nc.gpsimd.tensor_tensor(out=u[:, cols], in0=rows_first[i, "z"][:, cols], in1=u[:, cols], op=ALU.mult)

        def r_term_times_ghn(i):
            q_neg = rows_first_tile(i, "q_neg")
            nc.gpsimd.tensor_tensor(
                out=q_neg[:], in0=rows_first[i, "rt_neg"][:], in1=rows_first[i, "ghn"][:], op=ALU.mult
            )

        def transpose_f32(i, name, half):
            bank = banks.tile([P, PACK, P], F32, tag="bank")
            for t in range(PACK):
                col = half * K_PASS + t * P
                if name == "u" and half == 0:
                    nc.tensor.matmul(
                        out=bank[:, t, :],
                        lhsT=rows_first[i, "n"][:, col : col + P],
                        rhs=ident_f32[:],
                        is_transpose=True,
                        start=True,
                        stop=False,
                    )
                    nc.tensor.matmul(
                        out=bank[:, t, :],
                        lhsT=rows_first[i, "hp"][:, col : col + P],
                        rhs=minus_ident_bf16[:],
                        start=False,
                        stop=True,
                    )
                else:
                    nc.tensor.transpose(bank[:, t, :], rows_first[i, name][:, col : col + P], ident_f32[:])
            psum[i, name, half] = bank[:]

        def transpose_g(i):
            bank = banks.tile([P, HALVES * PACK, P], BF16, tag="bank")
            for chunk in range(HALVES * PACK):
                nc.tensor.transpose(
                    bank[:, chunk, :], rows_first[i, "g"][:, chunk * P : (chunk + 1) * P], ident_bf16[:]
                )
            psum[i, "g"] = bank[:]

        def from_psum(i, name, half):
            return psum[i, name, half].rearrange("p t b -> p b t")

        def k_first_tile(i, name, dtype):
            made = work.tile([P, HALVES, P, PACK], dtype, tag=name, name=name)
            k_first[i, name] = made
            return made

        def negate_g(i):
            g_neg = k_first_tile(i, "g_neg", BF16)
            nc.scalar.copy(out=g_neg[:], in_=psum[i, "g"].rearrange("p (h t) b -> p h b t", t=PACK))

        def product_a(i):
            a = k_first_tile(i, "a", F32)
            for half in range(HALVES):
                nc.vector.scalar_tensor_tensor(
                    out=a[:, half],
                    in0=from_psum(i, "z", half),
                    scalar=1.0,
                    in1=k_first[i, "g_neg"][:, half],
                    op0=ALU.subtract,
                    op1=ALU.mult,
                )

        def product_zt(i):
            zt = k_first_tile(i, "zt", F32)
            for half in (0,):
                nc.vector.tensor_tensor(
                    out=zt[:, half], in0=from_psum(i, "z", half), in1=k_first[i, "a"][:, half], op=ALU.mult
                )

        def dgi_tile(i):
            if (i, "dgi") not in k_first:
                dgi = work.tile([P, GATES, HALVES, P, PACK], BF16, align_bytes=64)
                k_first[i, "dgi"] = dgi

        def product_dz(i):
            dgi_tile(i)
            for half in range(HALVES):
                nc.vector.tensor_tensor(
                    out=k_first[i, "dgi"][:, 1, half], in0=from_psum(i, "u", half), in1=k_first[i, "zt" if half == 0 else "a"][:, half], op=ALU.mult
                )

        def product_dn(i):
            dgi_tile(i)
            dn_neg = k_first_tile(i, "dn_neg", F32)
            for half in range(HALVES):
                nc.vector.scalar_tensor_tensor(
                    out=dn_neg[:, half],
                    in0=from_psum(i, "n_sq", half),
                    scalar=1.0,
                    in1=k_first[i, "a"][:, half],
                    op0=ALU.subtract,
                    op1=ALU.mult,
                )

        def round_dn(i):
            nc.scalar.copy(
                out=k_first[i, "dgi"][:, 2].rearrange("p h b t -> p (h b t)"),
                in_=k_first[i, "dn_neg"][:].rearrange("p h b t -> p (h b t)"),
            )

        def product_dr(i):
            for half in range(HALVES):
                nc.vector.tensor_tensor(
                    out=k_first[i, "dgi"][:, 0, half],
                    in0=from_psum(i, "q_neg", half),
                    in1=k_first[i, "dn_neg"][:, half],
                    op=ALU.mult,
                )

        def quantise(i, first_gate, gate_count):
            if (i, "codes") not in k_first:
                codes = work.tile([P, PASSES * P], U32, align_bytes=64)
                scales = work.tile([P, PASSES * P], U8, align_bytes=64)
                k_first[i, "codes"] = codes
                k_first[i, "scales"] = scales
            first = first_gate * HALVES * P
            last = (first_gate + gate_count) * HALVES * P
            flat = k_first[i, "dgi"][:].rearrange("p j h b t -> p (j h b t)")
            nc.vector.quantize_mx(
                out=k_first[i, "codes"][:, first:last].bitcast(E5M2_X4),
                scales=k_first[i, "scales"][:, first:last],
                in_=flat[:, PACK * first : PACK * last],
            )

        def gpsimd_waits_for_quantise(i):
            seen = work.tile([P, 1], U32)
            nc.gpsimd.tensor_copy(out=seen[:], in_=k_first[i, "codes"][:, PASSES * P - 1 : PASSES * P])

        def multiply(i, run):
            gate = (run + 1) % GATES
            if run == 0:
                acc = sums.tile([P, N_MOVING], F32)
                psum[i, "acc"] = acc
            for c in range(gate * HALVES, (gate + 1) * HALVES):
                nc.tensor.matmul_mx(
                    out=psum[i, "acc"][:],
                    lhsT=k_first[i, "codes"][:, c * P : (c + 1) * P].bitcast(E5M2_X4),
                    lhsT_scale=k_first[i, "scales"][:, c * P : (c + 1) * P],
                    rhs=w_codes[:, c * L : c * L + N_MOVING].bitcast(E4M3_X4),
                    rhs_scale=w_scales[:, c * L : c * L + N_MOVING],
                    start=(run == 0 and c == gate * HALVES),
                    stop=(run == GATES - 1 and c == (gate + 1) * HALVES - 1),
                )

        def store(i):
            result = work.tile([P, L], F32)
            nc.scalar.copy(out=result[:], in_=psum[i, "acc"][:, 0:L])
            nc.scalar.dma_start(out=out[i * P : (i + 1) * P, :], in_=result[:])

        HEAD_ORDER = ("g", "z", "n", "hp", "r", "ghn")
        LOOP_ORDER = ("r", "g", "z", "hp", "n", "ghn")

        def transpose_both(i, name):
            for half in range(HALVES):
                transpose_f32(i, name, half)

        def quantise_tile(i):
            quantise(i, 0, 2)
            quantise(i, 2, 1)
            gpsimd_waits_for_quantise(i)

        load_weights()
        load(0, HEAD_ORDER)
        load(1, HEAD_ORDER)
        load(2, LOOP_ORDER)
        for c in range(PASSES):
            regroup_weights(c)
            if c >= 1:
                quantise_weights(c - 1)
        quantise_weights(PASSES - 1)

        transpose_g(0)
        negate_g(0)
        transpose_both(0, "z")
        square_n(0)
        transpose_both(0, "n_sq")
        state_minus_n(0)
        transpose_both(0, "u")
        r_term(0)
        r_term_times_ghn(0)
        product_a(0)
        product_zt(0)
        transpose_g(1)
        product_dn(0)
        round_dn(0)
        negate_g(1)
        transpose_both(1, "z")
        transpose_both(0, "q_neg")
        product_dz(0)
        load(3, LOOP_ORDER)
        state_minus_n(1)
        transpose_both(1, "u")
        square_n(1)
        product_a(1)
        product_zt(1)
        transpose_both(1, "n_sq")
        transpose_g(2)
        product_dr(0)
        r_term(1)
        quantise_tile(0)
        r_term_times_ghn(1)
        transpose_both(1, "q_neg")

        load(4, LOOP_ORDER)
        r_term(2)
        negate_g(2)
        state_minus_n(2)
        r_term_times_ghn(2)
        multiply(0, 0)
        product_dz(1)
        transpose_both(2, "z")
        multiply(0, 1)
        product_dn(1)
        round_dn(1)
        square_n(2)
        transpose_both(2, "u")
        multiply(0, 2)
        product_dr(1)
        transpose_both(2, "n_sq")
        transpose_f32(2, "q_neg", 0)

        for i in range(2, TOKEN_TILES):
            early = i == 2
            if live(i + 3):
                load(i + 3, LOOP_ORDER)
            if live(i + 1):
                r_term(i + 1)
            product_a(i)
            store(i - 2)
            if live(i + 1):
                square_n(i + 1)

            product_zt(i)
            if early:
                product_dz(i)
            quantise_tile(i - 1)
            if live(i + 1):
                state_minus_n(i + 1)
                r_term_times_ghn(i + 1)
            transpose_f32(i, "q_neg", 1)
            if live(i + 1):
                transpose_g(i + 1)
                negate_g(i + 1)
            multiply(i - 1, 0)

            if not early:
                product_dz(i)
            if live(i + 1):
                transpose_both(i + 1, "z")
            multiply(i - 1, 1)

            product_dn(i)
            if live(i + 1):
                transpose_both(i + 1, "u")
            multiply(i - 1, 2)
            if i == LAST:
                quantise(i, 1, 1)
                store(i - 1)
            round_dn(i)

            product_dr(i)
            if live(i + 1):
                transpose_both(i + 1, "n_sq")
                transpose_f32(i + 1, "q_neg", 0)

        quantise(LAST, 2, 1)
        multiply(LAST, 0)
        multiply(LAST, 1)
        quantise(LAST, 0, 1)
        multiply(LAST, 2)
        store(LAST)
